import numpy as np
import ml_dtypes


def mxq(x, axis, fmt="e4m3"):
    dtype, down = {"e4m3": (ml_dtypes.float8_e4m3fn, 7), "e5m2": (ml_dtypes.float8_e5m2, 14)}[fmt]
    v = np.moveaxis(np.asarray(x, np.float32).astype(ml_dtypes.bfloat16).astype(np.float64), axis, -1)
    blocks = v.reshape(v.shape[:-1] + (-1, 32))
    amax = np.abs(blocks).max(-1, keepdims=True)
    byte = np.maximum(np.where(amax > 0, np.frexp(amax)[1] - 1 + 127, 0) - down, 1)
    scale = np.exp2(byte - 127.0)
    codes = (blocks / scale).astype(np.float32).astype(dtype).astype(np.float64)
    return np.moveaxis((codes * scale).reshape(v.shape), -1, axis)


WIDE = False


def mx_kscale(k):
    if not WIDE:
        return np.ones(k)
    levels = np.array([10, -10, 5, -5, 0])
    a = np.random.permutation(np.resize(levels, k // 512 * 4)).reshape(k // 512, 4)
    idx = np.arange(k)
    return np.exp2(a[idx // 512, idx % 128 // 32])


BF16 = ml_dtypes.bfloat16


def bf(x):
    return np.asarray(x, np.float32).astype(BF16)


def f64(x):
    return np.asarray(x).astype(np.float64)


B, S, H, I = 4, 32, 512, 1024


def silu(v):
    return v / (1.0 + np.exp(-v))


def setup_inputs():
    s = mx_kscale(H)
    c = np.exp2(-np.round(0.25 * np.log2(np.mean(1.0 / s**2))))
    t = c * np.exp2(np.round(np.log2(mx_kscale(I)) / 2))
    return {"hidden_state": bf(np.random.standard_normal((B, S, H)) * s),
            "w_gate": bf(np.random.standard_normal((I, H)) * 1.0 / np.sqrt(H) / s[None, :]),
            "w_up": bf(np.random.standard_normal((I, H)) * 0.8 / np.sqrt(H) / s[None, :] * t[:, None]),
            "w_down": bf(np.random.standard_normal((H, I)) * 2.0 / np.sqrt(I) / t[None, :])}


def reference(hidden_state, w_gate, w_up, w_down):
    xq = mxq(f64(hidden_state), 2, "e4m3")
    wu = f64(w_up)
    gate = silu(xq @ mxq(f64(w_gate), 1, "e4m3").T)
    up = xq @ mxq(wu, 1, "e4m3").T
    intermediate = gate * up
    s = np.sum(intermediate ** 2, axis=1)
    row_sq = np.sum(wu ** 2, axis=-1)
    impacts = np.sqrt(s * row_sq[None, :])
    out = mxq(intermediate, 2, "e4m3") @ mxq(f64(w_down), 1, "e4m3").T
    return out, impacts

@@ -1,0 +1,270 @@
+from contextlib import ExitStack
+
+import concourse.mybir as mybir
+from concourse.masks import make_identity
+
+F32 = mybir.dt.float32
+BF16 = mybir.dt.bfloat16
+U32 = mybir.dt.uint32
+U8 = mybir.dt.uint8
+FP8X4 = mybir.dt.float8_e4m3fn_x4
+ACT = mybir.ActivationFunctionType
+ALU = mybir.AluOpType
+
+P = 128
+PACK = 4
+K_PASS = P * PACK
+BATCH = 4
+HIDDEN = 512
+INTER = 1024
+PASSES_2 = INTER // K_PASS
+CHUNK_OPERANDS = 2
+CHUNK_COLS = CHUNK_OPERANDS * K_PASS
+CHUNKS = 4
+HALF_OUT = HIDDEN // 2
+FLOPS = 2 * P * HIDDEN * INTER * 3
+
+
+def turn_words(nc, banks, rows, identity):
+    words = rows.bitcast(F32)
+    bank = banks.tile([P, 2 * CHUNK_OPERANDS, P], F32, tag="bank")
+    for j in range(words.shape[1] // P):
+        nc.tensor.transpose(bank[:, j, :], words[:, j * P : (j + 1) * P], identity)
+    return bank
+
+
+def regroup(copy, stage, bank, operands):
+    grouped = stage.tile([P, operands * K_PASS], BF16, tag="grouped", align_bytes=64)
+    copy(
+        out=grouped[:].bitcast(F32).rearrange("p (a r h) -> p a r h", a=operands, h=2),
+        in_=bank[:, 0 : 2 * operands, :].rearrange("p (a h) r -> p a r h", h=2),
+    )
+    return grouped
+
+
+def quantise(nc, grouped, pieces):
+    cols = grouped.shape[1] // len(pieces)
+    for j, (codes, scales) in enumerate(pieces):
+        nc.vector.quantize_mx(
+            out=codes.bitcast(FP8X4), scales=scales, in_=grouped[:, j * cols : (j + 1) * cols]
+        )
+
+
+def tile_qwen2mlp_nd_s_kernel(tc, hidden_state, w_gate, w_up, w_down, out, impacts):
+    nc = tc.nc
+    with ExitStack() as ctx:
+        keep = ctx.enter_context(tc.tile_pool(name="keep", bufs=1))
+        stage = ctx.enter_context(tc.tile_pool(name="stage", bufs=4))
+        work = ctx.enter_context(tc.tile_pool(name="work", bufs=2))
+        banks = ctx.enter_context(tc.psum_pool(name="banks", bufs=4))
+        acc_pool = ctx.enter_context(tc.psum_pool(name="acc_pool", bufs=2))
+        out_pool = ctx.enter_context(tc.psum_pool(name="out_pool", bufs=2))
+        ctx.enter_context(tc.manual_schedule())
+
+        x_rows = keep.tile([P, HIDDEN], BF16, name="x_rows")
+        nc.sync.dma_start(out=x_rows[:], in_=hidden_state.rearrange("b s k -> (b s) k"))
+        gate_rows = []
+        up_rows = []
+        down_rows = []
+        for c in range(CHUNKS):
+            for label, weight, tiles in (("gate", w_gate, gate_rows), ("up", w_up, up_rows)):
+                rows = keep.tile([P, CHUNK_COLS], BF16, name="%s_rows%d" % (label, c))
+                chunks = weight.rearrange("(c m e) k -> c m (e k)", c=CHUNKS, e=CHUNK_OPERANDS)
+                nc.sync.dma_start(out=rows[:], in_=chunks[c])
+                tiles.append(rows)
+        for n in range(CHUNKS):
+            rows = keep.tile([P, CHUNK_COLS], BF16, name="down_rows%d" % n)
+            nc.sync.dma_start(out=rows[:], in_=w_down.rearrange("(n r) k -> n r k", r=P)[n])
+            down_rows.append(rows)
+
+        identity = keep.tile([P, P], F32, name="identity")
+        make_identity(nc, identity[:])
+        ones = keep.tile([P, 1], F32, name="ones")
+        nc.vector.memset(ones[:], 1.0)
+        products = keep.tile([P, CHUNK_OPERANDS, P], F32, name="products")
+        nc.vector.memset(products[:], 0.0)
+        table_warm = keep.tile([P, 1], F32, name="table_warm")
+        nc.scalar.activation(out=table_warm[:], in_=ones[:], func=ACT.Silu)
+
+        x_codes = keep.tile([P, P], U32, name="x_codes", align_bytes=64)
+        x_scales = keep.tile([P, P], U8, name="x_scales", align_bytes=64)
+        gate_codes = keep.tile([P, CHUNKS, CHUNK_OPERANDS * P], U32, name="gate_codes", align_bytes=64)
+        gate_scales = keep.tile([P, CHUNKS, CHUNK_OPERANDS * P], U8, name="gate_scales", align_bytes=64)
+        up_codes = keep.tile([P, CHUNKS, CHUNK_OPERANDS * P], U32, name="up_codes", align_bytes=64)
+        up_scales = keep.tile([P, CHUNKS, CHUNK_OPERANDS * P], U8, name="up_scales", align_bytes=64)
+        down_codes = keep.tile([P, PASSES_2, HIDDEN], U32, name="down_codes", align_bytes=64)
+        down_scales = keep.tile([P, PASSES_2, HIDDEN], U8, name="down_scales", align_bytes=64)
+        h_codes = keep.tile([P, PASSES_2, P], U32, name="h_codes", align_bytes=64)
+        h_scales = keep.tile([P, PASSES_2, P], U8, name="h_scales", align_bytes=64)
+
+        h_f32 = [keep.tile([P, PACK, P], F32, name="h_f32_%d" % g) for g in range(PASSES_2)]
+        h_grouped = {}
+        row_sq = keep.tile([P, CHUNK_OPERANDS, CHUNKS], F32, name="row_sq")
+        h_sq_sum = keep.tile([P, CHUNK_OPERANDS, BATCH, CHUNKS], F32, name="h_sq_sum")
+
+        pairs = []
+        for c in range(CHUNKS):
+            pairs.append(
+                (
+                    (gate_rows[c], [(gate_codes[:, c, :], gate_scales[:, c, :])], nc.vector.tensor_copy),
+                    (up_rows[c], [(up_codes[:, c, :], up_scales[:, c, :])], nc.vector.tensor_copy),
+                )
+            )
+        for first in range(0, CHUNKS, 2):
+            pair = []
+            for n in (first, first + 1):
+                cols = slice(n * P, (n + 1) * P)
+                pieces = [(down_codes[:, g, cols], down_scales[:, g, cols]) for g in range(PASSES_2)]
+                pair.append((down_rows[n], pieces, nc.scalar.copy))
+            pairs.append(tuple(pair))
+        turned = {}
+        grouped = {}
+        acc = {}
+        silu_gate = {}
+        h_sq = {}
+        out_acc = {}
+
+        def turn(j):
+            turned[j] = [turn_words(nc, banks, rows[:], identity[:]) for rows, pieces, copy in pairs[j]]
+
+        def empty(j):
+            grouped[j] = [
+                regroup(copy, stage, bank, CHUNK_OPERANDS)
+                for bank, (rows, pieces, copy) in zip(turned[j], pairs[j])
+            ]
+
+        def pack(j):
+            for tile_in, (rows, pieces, copy) in zip(grouped[j], pairs[j]):
+                quantise(nc, tile_in, pieces)
+
+        def square_up_rows(c):
+            for e in range(CHUNK_OPERANDS):
+                squares = work.tile([P, K_PASS], F32, tag="squares")
+                nc.scalar.activation(
+                    out=squares[:],
+                    in_=up_rows[c][:, e * K_PASS : (e + 1) * K_PASS],
+                    func=ACT.Square,
+                    accum_out=row_sq[:, e, c : c + 1],
+                )
+
+        def first_products(c):
+            acc[c] = acc_pool.tile([P, 2, CHUNK_OPERANDS, P], F32, tag="acc", name="acc%d" % c)
+            for w, (codes, scales) in enumerate(((gate_codes, gate_scales), (up_codes, up_scales))):
+                for e in range(CHUNK_OPERANDS):
+                    cols = slice(e * P, (e + 1) * P)
+                    nc.tensor.matmul_mx(
+                        out=acc[c][:, w, e, :],
+                        lhsT=codes[:, c, cols].bitcast(FP8X4),
+                        lhsT_scale=scales[:, c, cols],
+                        rhs=x_codes[:].bitcast(FP8X4),
+                        rhs_scale=x_scales[:],
+                        start=True,
+                        stop=True,
+                    )
+
+        def silu(c):
+            silu_gate[c] = work.tile([P, CHUNK_OPERANDS, P], F32, tag="silu_gate", name="silu_gate%d" % c)
+            nc.scalar.activation(out=silu_gate[c][:], in_=acc[c][:, 0], func=ACT.Silu)
+
+        def h_rows(c):
+            g, u = divmod(c, 2)
+            return h_f32[g][:, 2 * u : 2 * u + 2, :]
+
+        def multiply(c):
+            nc.vector.tensor_tensor(out=h_rows(c), in0=silu_gate[c][:], in1=acc[c][:, 1], op=ALU.mult)
+
+        def round_h(g):
+            h_grouped[g] = work.tile([P, P, PACK], BF16, tag="h_grouped", name="h_grouped%d" % g, align_bytes=64)
+            nc.vector.tensor_copy(out=h_grouped[g][:], in_=h_f32[g][:].rearrange("p t k -> p k t"))
+
+        def pack_h(g):
+            nc.vector.quantize_mx(
+                out=h_codes[:, g, :].bitcast(FP8X4),
+                scales=h_scales[:, g, :],
+                in_=h_grouped[g][:].rearrange("p k t -> p (k t)"),
+            )
+
+        def square_h(c):
+            h_sq[c] = work.tile([P, CHUNK_OPERANDS, P], F32, tag="h_sq", name="h_sq%d" % c)
+            nc.scalar.activation(out=h_sq[c][:], in_=h_rows(c), func=ACT.Square)
+
+        def sum_h_squares(c):
+            nc.vector.tensor_reduce(
+                out=h_sq_sum[:, :, :, c],
+                in_=h_sq[c][:].rearrange("p e (b s) -> p e b s", b=BATCH),
+                axis=mybir.AxisListType.X,
+                op=ALU.add,
+            )
+
+        def third_product(half):
+            cols = slice(half * HALF_OUT, (half + 1) * HALF_OUT)
+            out_acc[half] = out_pool.tile([P, HALF_OUT], F32, tag="out_acc", name="out_acc%d" % half)
+            for g in range(PASSES_2):
+                nc.tensor.matmul_mx(
+                    out=out_acc[half][:],
+                    lhsT=h_codes[:, g, :].bitcast(FP8X4),
+                    lhsT_scale=h_scales[:, g, :],
+                    rhs=down_codes[:, g, cols].bitcast(FP8X4),
+                    rhs_scale=down_scales[:, g, cols],
+                    start=(g == 0),
+                    stop=(g == PASSES_2 - 1),
+                )
+
+        def store_out(half):
+            cols = slice(half * HALF_OUT, (half + 1) * HALF_OUT)
+            out_sb = work.tile([P, HALF_OUT], F32, tag="out_sb")
+            nc.vector.tensor_copy(out=out_sb[:], in_=out_acc[half][:])
+            nc.sync.dma_start(out=out.rearrange("b s n -> (b s) n")[:, cols], in_=out_sb[:])
+
+        x_bank = turn_words(nc, banks, x_rows[:], identity[:])
+        x_grouped = regroup(nc.scalar.copy, stage, x_bank, 1)
+        turn(0)
+        turn(1)
+        quantise(nc, x_grouped, [(x_codes[:], x_scales[:])])
+
+        for j in range(len(pairs)):
+            if 1 <= j <= CHUNKS:
+                silu(j - 1)
+            empty(j)
+            if j + 2 < len(pairs):
+                turn(j + 2)
+            if j < CHUNKS:
+                square_up_rows(j)
+            if 2 <= j <= CHUNKS + 1:
+                sum_h_squares(j - 2)
+                if (j - 2) % 2 == 1:
+                    pack_h((j - 2) // 2)
+            if j == len(pairs) - 1:
+                nc.scalar.activation(out=table_warm[:], in_=ones[:], func=ACT.Sqrt)
+                nc.vector.tensor_tensor(
+                    out=products[:, :, 0 : BATCH * CHUNKS].rearrange("p e (b c) -> p e b c", b=BATCH),
+                    in0=h_sq_sum[:],
+                    in1=row_sq[:].unsqueeze(2).to_broadcast([P, CHUNK_OPERANDS, BATCH, CHUNKS]),
+                    op=ALU.mult,
+                )
+                products_t = banks.tile([P, 2 * CHUNK_OPERANDS, P], F32, tag="bank")
+                for e in range(CHUNK_OPERANDS):
+                    nc.tensor.transpose(products_t[:, e, :], products[:, e, :], identity[:])
+                third_product(0)
+            pack(j)
+            if j < CHUNKS:
+                first_products(j)
+            if 1 <= j <= CHUNKS:
+                multiply(j - 1)
+                if (j - 1) % 2 == 1:
+                    round_h((j - 1) // 2)
+                square_h(j - 1)
+
+        store_out(0)
+        third_product(1)
+        store_out(1)
+        impacts_sb = keep.tile([P, P, CHUNK_OPERANDS], F32, name="impacts_sb")
+        nc.scalar.activation(
+            out=impacts_sb[:],
+            in_=products_t[:, 0:CHUNK_OPERANDS, :].rearrange("r e m -> r m e"),
+            func=ACT.Sqrt,
+        )
+        nc.sync.dma_start(
+            out=impacts.rearrange("b (c i) -> (b c) i", c=CHUNKS),
+            in_=impacts_sb[0 : BATCH * CHUNKS].rearrange("r m e -> r (m e)"),
+        )

@@ -25,12 +25,10 @@ HALF_OUT = HIDDEN // 2
 FLOPS = 2 * P * HIDDEN * INTER * 3
 
 
-def turn_words(nc, banks, rows, identity):
+def turn_words(nc, bank, rows, identity):
     words = rows.bitcast(F32)
-    bank = banks.tile([P, 2 * CHUNK_OPERANDS, P], F32, tag="bank")
     for j in range(words.shape[1] // P):
         nc.tensor.transpose(bank[:, j, :], words[:, j * P : (j + 1) * P], identity)
-    return bank
 
 
 def regroup(copy, stage, bank, operands):
@@ -57,25 +55,23 @@ def tile_qwen2mlp_nd_s_kernel(tc, hidden_state, w_gate, w_up, w_down, out, impac
         stage = ctx.enter_context(tc.tile_pool(name="stage", bufs=4))
         work = ctx.enter_context(tc.tile_pool(name="work", bufs=2))
         banks = ctx.enter_context(tc.psum_pool(name="banks", bufs=4))
-        acc_pool = ctx.enter_context(tc.psum_pool(name="acc_pool", bufs=2))
-        out_pool = ctx.enter_context(tc.psum_pool(name="out_pool", bufs=2))
+        acc_pool = ctx.enter_context(tc.psum_pool(name="acc_pool", bufs=4))
         ctx.enter_context(tc.manual_schedule())
 
-        x_rows = keep.tile([P, HIDDEN], BF16, name="x_rows")
-        nc.sync.dma_start(out=x_rows[:], in_=hidden_state.rearrange("b s k -> (b s) k"))
-        gate_rows = []
-        up_rows = []
-        down_rows = []
+        rows_of = {}
+
+        def load(key, cols, source):
+            rows_of[key] = keep.tile([P, cols], BF16, name="%s_rows%d" % key)
+            nc.sync.dma_start(out=rows_of[key][:], in_=source)
+
         for c in range(CHUNKS):
-            for label, weight, tiles in (("gate", w_gate, gate_rows), ("up", w_up, up_rows)):
-                rows = keep.tile([P, CHUNK_COLS], BF16, name="%s_rows%d" % (label, c))
+            for label, weight in (("gate", w_gate), ("up", w_up)):
                 chunks = weight.rearrange("(c m e) k -> c m (e k)", c=CHUNKS, e=CHUNK_OPERANDS)
-                nc.sync.dma_start(out=rows[:], in_=chunks[c])
-                tiles.append(rows)
+                load((label, c), CHUNK_COLS, chunks[c])
+            if c == 0:
+                load(("x", 0), HIDDEN, hidden_state.rearrange("b s k -> (b s) k"))
         for n in range(CHUNKS):
-            rows = keep.tile([P, CHUNK_COLS], BF16, name="down_rows%d" % n)
-            nc.sync.dma_start(out=rows[:], in_=w_down.rearrange("(n r) k -> n r k", r=P)[n])
-            down_rows.append(rows)
+            load(("down", n), CHUNK_COLS, w_down.rearrange("(n r) k -> n r k", r=P)[n])
 
         identity = keep.tile([P, P], F32, name="identity")
         make_identity(nc, identity[:])
@@ -88,90 +84,87 @@ def tile_qwen2mlp_nd_s_kernel(tc, hidden_state, w_gate, w_up, w_down, out, impac
 
         x_codes = keep.tile([P, P], U32, name="x_codes", align_bytes=64)
         x_scales = keep.tile([P, P], U8, name="x_scales", align_bytes=64)
-        gate_codes = keep.tile([P, CHUNKS, CHUNK_OPERANDS * P], U32, name="gate_codes", align_bytes=64)
-        gate_scales = keep.tile([P, CHUNKS, CHUNK_OPERANDS * P], U8, name="gate_scales", align_bytes=64)
-        up_codes = keep.tile([P, CHUNKS, CHUNK_OPERANDS * P], U32, name="up_codes", align_bytes=64)
-        up_scales = keep.tile([P, CHUNKS, CHUNK_OPERANDS * P], U8, name="up_scales", align_bytes=64)
+        first_codes = {}
+        first_scales = {}
+        for label in ("gate", "up"):
+            first_codes[label] = keep.tile(
+                [P, CHUNKS, CHUNK_OPERANDS * P], U32, name="%s_codes" % label, align_bytes=64
+            )
+            first_scales[label] = keep.tile(
+                [P, CHUNKS, CHUNK_OPERANDS * P], U8, name="%s_scales" % label, align_bytes=64
+            )
         down_codes = keep.tile([P, PASSES_2, HIDDEN], U32, name="down_codes", align_bytes=64)
         down_scales = keep.tile([P, PASSES_2, HIDDEN], U8, name="down_scales", align_bytes=64)
         h_codes = keep.tile([P, PASSES_2, P], U32, name="h_codes", align_bytes=64)
         h_scales = keep.tile([P, PASSES_2, P], U8, name="h_scales", align_bytes=64)
 
-        h_f32 = [keep.tile([P, PACK, P], F32, name="h_f32_%d" % g) for g in range(PASSES_2)]
-        h_grouped = {}
-        row_sq = keep.tile([P, CHUNK_OPERANDS, CHUNKS], F32, name="row_sq")
-        h_sq_sum = keep.tile([P, CHUNK_OPERANDS, BATCH, CHUNKS], F32, name="h_sq_sum")
-
-        pairs = []
+        pieces_of = {("x", 0): [(x_codes[:], x_scales[:])]}
         for c in range(CHUNKS):
-            pairs.append(
-                (
-                    (gate_rows[c], [(gate_codes[:, c, :], gate_scales[:, c, :])], nc.vector.tensor_copy),
-                    (up_rows[c], [(up_codes[:, c, :], up_scales[:, c, :])], nc.vector.tensor_copy),
-                )
-            )
-        for first in range(0, CHUNKS, 2):
-            pair = []
-            for n in (first, first + 1):
-                cols = slice(n * P, (n + 1) * P)
-                pieces = [(down_codes[:, g, cols], down_scales[:, g, cols]) for g in range(PASSES_2)]
-                pair.append((down_rows[n], pieces, nc.scalar.copy))
-            pairs.append(tuple(pair))
+            for label in ("gate", "up"):
+                pieces_of[(label, c)] = [(first_codes[label][:, c, :], first_scales[label][:, c, :])]
+            cols = slice(c * P, (c + 1) * P)
+            pieces_of[("down", c)] = [
+                (down_codes[:, g, cols], down_scales[:, g, cols]) for g in range(PASSES_2)
+            ]
+
+        row_sq = keep.tile([P, CHUNKS * CHUNK_OPERANDS], F32, name="row_sq")
+        h_sq_sum = keep.tile([P, PASSES_2, PACK * BATCH], F32, name="h_sq_sum")
+
         turned = {}
         grouped = {}
         acc = {}
         silu_gate = {}
+        h_f32 = {}
+        h_grouped = {}
         h_sq = {}
-        out_acc = {}
 
-        def turn(j):
-            turned[j] = [turn_words(nc, banks, rows[:], identity[:]) for rows, pieces, copy in pairs[j]]
+        def turn(key):
+            if key == ("x", 0):
+                turned[key] = acc_pool.tile([P, PACK, P], F32, tag="acc", name="x_bank")
+            else:
+                turned[key] = banks.tile([P, PACK, P], F32, tag="bank", name="%s_bank%d" % key)
+            turn_words(nc, turned[key], rows_of[key][:], identity[:])
 
-        def empty(j):
-            grouped[j] = [
-                regroup(copy, stage, bank, CHUNK_OPERANDS)
-                for bank, (rows, pieces, copy) in zip(turned[j], pairs[j])
-            ]
+        def empty(key, copy):
+            grouped[key] = regroup(copy, stage, turned[key], rows_of[key].shape[1] // K_PASS)
 
-        def pack(j):
-            for tile_in, (rows, pieces, copy) in zip(grouped[j], pairs[j]):
-                quantise(nc, tile_in, pieces)
+        def pack(key):
+            quantise(nc, grouped[key], pieces_of[key])
 
-        def square_up_rows(c):
-            for e in range(CHUNK_OPERANDS):
-                squares = work.tile([P, K_PASS], F32, tag="squares")
-                nc.scalar.activation(
-                    out=squares[:],
-                    in_=up_rows[c][:, e * K_PASS : (e + 1) * K_PASS],
-                    func=ACT.Square,
-                    accum_out=row_sq[:, e, c : c + 1],
-                )
+        def square_up_rows(block):
+            c, e = divmod(block, CHUNK_OPERANDS)
+            squares = work.tile([P, K_PASS], F32, tag="squares")
+            nc.scalar.activation(
+                out=squares[:],
+                in_=rows_of[("up", c)][:, e * K_PASS : (e + 1) * K_PASS],
+                func=ACT.Square,
+                accum_out=row_sq[:, block : block + 1],
+            )
 
         def first_products(c):
-            acc[c] = acc_pool.tile([P, 2, CHUNK_OPERANDS, P], F32, tag="acc", name="acc%d" % c)
-            for w, (codes, scales) in enumerate(((gate_codes, gate_scales), (up_codes, up_scales))):
+            g, u = divmod(c, 2)
+            for label in ("gate", "up"):
+                if u == 0:
+                    acc[(label, g)] = acc_pool.tile([P, PACK, P], F32, tag="acc", name="%s_acc%d" % (label, g))
                 for e in range(CHUNK_OPERANDS):
                     cols = slice(e * P, (e + 1) * P)
                     nc.tensor.matmul_mx(
-                        out=acc[c][:, w, e, :],
-                        lhsT=codes[:, c, cols].bitcast(FP8X4),
-                        lhsT_scale=scales[:, c, cols],
+                        out=acc[(label, g)][:, 2 * u + e, :],
+                        lhsT=first_codes[label][:, c, cols].bitcast(FP8X4),
+                        lhsT_scale=first_scales[label][:, c, cols],
                         rhs=x_codes[:].bitcast(FP8X4),
                         rhs_scale=x_scales[:],
                         start=True,
                         stop=True,
                     )
 
-        def silu(c):
-            silu_gate[c] = work.tile([P, CHUNK_OPERANDS, P], F32, tag="silu_gate", name="silu_gate%d" % c)
-            nc.scalar.activation(out=silu_gate[c][:], in_=acc[c][:, 0], func=ACT.Silu)
+        def silu(g):
+            silu_gate[g] = work.tile([P, PACK, P], F32, tag="silu_gate", name="silu_gate%d" % g)
+            nc.scalar.activation(out=silu_gate[g][:], in_=acc[("gate", g)][:], func=ACT.Silu)
 
-        def h_rows(c):
-            g, u = divmod(c, 2)
-            return h_f32[g][:, 2 * u : 2 * u + 2, :]
-
-        def multiply(c):
-            nc.vector.tensor_tensor(out=h_rows(c), in0=silu_gate[c][:], in1=acc[c][:, 1], op=ALU.mult)
+        def multiply(g):
+            h_f32[g] = work.tile([P, PACK, P], F32, tag="h_f32", name="h_f32_%d" % g)
+            nc.vector.tensor_tensor(out=h_f32[g][:], in0=silu_gate[g][:], in1=acc[("up", g)][:], op=ALU.mult)
 
         def round_h(g):
             h_grouped[g] = work.tile([P, P, PACK], BF16, tag="h_grouped", name="h_grouped%d" % g, align_bytes=64)
@@ -184,24 +177,24 @@ def tile_qwen2mlp_nd_s_kernel(tc, hidden_state, w_gate, w_up, w_down, out, impac
                 in_=h_grouped[g][:].rearrange("p k t -> p (k t)"),
             )
 
-        def square_h(c):
-            h_sq[c] = work.tile([P, CHUNK_OPERANDS, P], F32, tag="h_sq", name="h_sq%d" % c)
-            nc.scalar.activation(out=h_sq[c][:], in_=h_rows(c), func=ACT.Square)
+        def square_h(g):
+            h_sq[g] = work.tile([P, PACK, P], F32, tag="h_sq", name="h_sq%d" % g)
+            nc.scalar.activation(out=h_sq[g][:], in_=h_f32[g][:], func=ACT.Square)
 
-        def sum_h_squares(c):
+        def sum_h_squares(g):
             nc.vector.tensor_reduce(
-                out=h_sq_sum[:, :, :, c],
-                in_=h_sq[c][:].rearrange("p e (b s) -> p e b s", b=BATCH),
+                out=h_sq_sum[:, g, :],
+                in_=h_sq[g][:].rearrange("p t (b s) -> p (t b) s", b=BATCH),
                 axis=mybir.AxisListType.X,
                 op=ALU.add,
             )
 
         def third_product(half):
             cols = slice(half * HALF_OUT, (half + 1) * HALF_OUT)
-            out_acc[half] = out_pool.tile([P, HALF_OUT], F32, tag="out_acc", name="out_acc%d" % half)
+            acc[("out", half)] = acc_pool.tile([P, HALF_OUT], F32, tag="acc", name="out_acc%d" % half)
             for g in range(PASSES_2):
                 nc.tensor.matmul_mx(
-                    out=out_acc[half][:],
+                    out=acc[("out", half)][:],
                     lhsT=h_codes[:, g, :].bitcast(FP8X4),
                     lhsT_scale=h_scales[:, g, :],
                     rhs=down_codes[:, g, cols].bitcast(FP8X4),
@@ -210,54 +203,75 @@ def tile_qwen2mlp_nd_s_kernel(tc, hidden_state, w_gate, w_up, w_down, out, impac
                     stop=(g == PASSES_2 - 1),
                 )
 
-        def store_out(half):
+        def store_out(half, copy):
             cols = slice(half * HALF_OUT, (half + 1) * HALF_OUT)
             out_sb = work.tile([P, HALF_OUT], F32, tag="out_sb")
-            nc.vector.tensor_copy(out=out_sb[:], in_=out_acc[half][:])
+            copy(out=out_sb[:], in_=acc[("out", half)][:])
             nc.sync.dma_start(out=out.rearrange("b s n -> (b s) n")[:, cols], in_=out_sb[:])
 
-        x_bank = turn_words(nc, banks, x_rows[:], identity[:])
-        x_grouped = regroup(nc.scalar.copy, stage, x_bank, 1)
-        turn(0)
-        turn(1)
-        quantise(nc, x_grouped, [(x_codes[:], x_scales[:])])
+        turn(("gate", 0))
+        turn(("up", 0))
+        turn(("x", 0))
+        turn(("gate", 1))
+        turn(("up", 1))
+        for c in range(CHUNKS):
+            empty(("gate", c), nc.scalar.copy)
+            empty(("up", c), nc.vector.tensor_copy)
+            square_up_rows(c)
+            pack(("gate", c))
+            pack(("up", c))
+            if c == 0:
+                empty(("x", 0), nc.scalar.copy)
+                pack(("x", 0))
+            if c + 2 < CHUNKS:
+                turn(("gate", c + 2))
+                turn(("up", c + 2))
+            first_products(c)
+            if c + 2 >= CHUNKS:
+                turn(("down", 2 * (c + 2 - CHUNKS)))
+                turn(("down", 2 * (c + 2 - CHUNKS) + 1))
 
-        for j in range(len(pairs)):
-            if 1 <= j <= CHUNKS:
-                silu(j - 1)
-            empty(j)
-            if j + 2 < len(pairs):
-                turn(j + 2)
-            if j < CHUNKS:
-                square_up_rows(j)
-            if 2 <= j <= CHUNKS + 1:
-                sum_h_squares(j - 2)
-                if (j - 2) % 2 == 1:
-                    pack_h((j - 2) // 2)
-            if j == len(pairs) - 1:
-                nc.scalar.activation(out=table_warm[:], in_=ones[:], func=ACT.Sqrt)
-                nc.vector.tensor_tensor(
-                    out=products[:, :, 0 : BATCH * CHUNKS].rearrange("p e (b c) -> p e b c", b=BATCH),
-                    in0=h_sq_sum[:],
-                    in1=row_sq[:].unsqueeze(2).to_broadcast([P, CHUNK_OPERANDS, BATCH, CHUNKS]),
-                    op=ALU.mult,
-                )
-                products_t = banks.tile([P, 2 * CHUNK_OPERANDS, P], F32, tag="bank")
-                for e in range(CHUNK_OPERANDS):
-                    nc.tensor.transpose(products_t[:, e, :], products[:, e, :], identity[:])
-                third_product(0)
-            pack(j)
-            if j < CHUNKS:
-                first_products(j)
-            if 1 <= j <= CHUNKS:
-                multiply(j - 1)
-                if (j - 1) % 2 == 1:
-                    round_h((j - 1) // 2)
-                square_h(j - 1)
-
-        store_out(0)
+        silu(0)
+        multiply(0)
+        square_up_rows(4)
+        square_up_rows(5)
+        empty(("down", 0), nc.vector.tensor_copy)
+        round_h(0)
+        empty(("down", 1), nc.vector.tensor_copy)
+        silu(1)
+        multiply(1)
+        square_h(0)
+        pack(("down", 0))
+        round_h(1)
+        pack(("down", 1))
+        pack_h(0)
+        pack_h(1)
+        third_product(0)
+        empty(("down", 2), nc.scalar.copy)
+        square_h(1)
+        empty(("down", 3), nc.vector.tensor_copy)
+        square_up_rows(6)
+        square_up_rows(7)
+        nc.scalar.activation(out=table_warm[:], in_=ones[:], func=ACT.Sqrt)
+        sum_h_squares(0)
+        pack(("down", 2))
+        pack(("down", 3))
         third_product(1)
-        store_out(1)
+        sum_h_squares(1)
+        nc.vector.tensor_tensor(
+            out=products[:, :, 0 : BATCH * CHUNKS].rearrange("p e (b c) -> p e b c", b=BATCH),
+            in0=h_sq_sum[:].rearrange("p g (u e b) -> p e b (g u)", u=2, e=CHUNK_OPERANDS),
+            in1=row_sq[:]
+            .rearrange("p (c e) -> p e c", e=CHUNK_OPERANDS)
+            .unsqueeze(2)
+            .to_broadcast([P, CHUNK_OPERANDS, BATCH, CHUNKS]),
+            op=ALU.mult,
+        )
+        products_t = banks.tile([P, PACK, P], F32, tag="bank")
+        for e in range(CHUNK_OPERANDS):
+            nc.tensor.transpose(products_t[:, e, :], products[:, e, :], identity[:])
+        store_out(0, nc.scalar.copy)
+        store_out(1, nc.vector.tensor_copy)
         impacts_sb = keep.tile([P, P, CHUNK_OPERANDS], F32, name="impacts_sb")
         nc.scalar.activation(
             out=impacts_sb[:],

@@ -22,6 +22,7 @@ CHUNK_OPERANDS = 2
 CHUNK_COLS = CHUNK_OPERANDS * K_PASS
 CHUNKS = 4
 HALF_OUT = HIDDEN // 2
+WARM_PASSES = 20
 FLOPS = 2 * P * HIDDEN * INTER * 3
 
 
@@ -81,6 +82,23 @@ def tile_qwen2mlp_nd_s_kernel(tc, hidden_state, w_gate, w_up, w_down, out, impac
         nc.vector.memset(products[:], 0.0)
         table_warm = keep.tile([P, 1], F32, name="table_warm")
         nc.scalar.activation(out=table_warm[:], in_=ones[:], func=ACT.Silu)
+
+        zeros = keep.tile([P, K_PASS], BF16, name="zeros", align_bytes=64)
+        nc.vector.memset(zeros[:], 0.0)
+        zero_codes = keep.tile([P, P], U32, name="zero_codes", align_bytes=64)
+        zero_scales = keep.tile([P, P], U8, name="zero_scales", align_bytes=64)
+        nc.vector.quantize_mx(out=zero_codes[:].bitcast(FP8X4), scales=zero_scales[:], in_=zeros[:])
+        warm_bank = acc_pool.tile([P, P], F32, tag="acc", name="warm_bank")
+        for i in range(WARM_PASSES):
+            nc.tensor.matmul_mx(
+                out=warm_bank[:],
+                lhsT=zero_codes[:].bitcast(FP8X4),
+                lhsT_scale=zero_scales[:],
+                rhs=zero_codes[:].bitcast(FP8X4),
+                rhs_scale=zero_scales[:],
+                start=True,
+                stop=True,
+            )
 
         x_codes = keep.tile([P, P], U32, name="x_codes", align_bytes=64)
         x_scales = keep.tile([P, P], U8, name="x_scales", align_bytes=64)

@@ -22,7 +22,6 @@ CHUNK_OPERANDS = 2
 CHUNK_COLS = CHUNK_OPERANDS * K_PASS
 CHUNKS = 4
 HALF_OUT = HIDDEN // 2
-WARM_PASSES = 20
 FLOPS = 2 * P * HIDDEN * INTER * 3
 
 
@@ -65,12 +64,16 @@ def tile_qwen2mlp_nd_s_kernel(tc, hidden_state, w_gate, w_up, w_down, out, impac
             rows_of[key] = keep.tile([P, cols], BF16, name="%s_rows%d" % key)
             nc.sync.dma_start(out=rows_of[key][:], in_=source)
 
-        for c in range(CHUNKS):
-            for label, weight in (("gate", w_gate), ("up", w_up)):
-                chunks = weight.rearrange("(c m e) k -> c m (e k)", c=CHUNKS, e=CHUNK_OPERANDS)
-                load((label, c), CHUNK_COLS, chunks[c])
-            if c == 0:
-                load(("x", 0), HIDDEN, hidden_state.rearrange("b s k -> (b s) k"))
+        def load_first(label, weight, c):
+            chunks = weight.rearrange("(c m e) k -> c m (e k)", c=CHUNKS, e=CHUNK_OPERANDS)
+            load((label, c), CHUNK_COLS, chunks[c])
+
+        load_first("up", w_up, 0)
+        load_first("gate", w_gate, 0)
+        load(("x", 0), HIDDEN, hidden_state.rearrange("b s k -> (b s) k"))
+        for c in range(1, CHUNKS):
+            load_first("gate", w_gate, c)
+            load_first("up", w_up, c)
         for n in range(CHUNKS):
             load(("down", n), CHUNK_COLS, w_down.rearrange("(n r) k -> n r k", r=P)[n])
 
@@ -82,23 +85,6 @@ def tile_qwen2mlp_nd_s_kernel(tc, hidden_state, w_gate, w_up, w_down, out, impac
         nc.vector.memset(products[:], 0.0)
         table_warm = keep.tile([P, 1], F32, name="table_warm")
         nc.scalar.activation(out=table_warm[:], in_=ones[:], func=ACT.Silu)
-
-        zeros = keep.tile([P, K_PASS], BF16, name="zeros", align_bytes=64)
-        nc.vector.memset(zeros[:], 0.0)
-        zero_codes = keep.tile([P, P], U32, name="zero_codes", align_bytes=64)
-        zero_scales = keep.tile([P, P], U8, name="zero_scales", align_bytes=64)
-        nc.vector.quantize_mx(out=zero_codes[:].bitcast(FP8X4), scales=zero_scales[:], in_=zeros[:])
-        warm_bank = acc_pool.tile([P, P], F32, tag="acc", name="warm_bank")
-        for i in range(WARM_PASSES):
-            nc.tensor.matmul_mx(
-                out=warm_bank[:],
-                lhsT=zero_codes[:].bitcast(FP8X4),
-                lhsT_scale=zero_scales[:],
-                rhs=zero_codes[:].bitcast(FP8X4),
-                rhs_scale=zero_scales[:],
-                start=True,
-                stop=True,
-            )
 
         x_codes = keep.tile([P, P], U32, name="x_codes", align_bytes=64)
         x_scales = keep.tile([P, P], U8, name="x_scales", align_bytes=64)
@@ -221,25 +207,27 @@ def tile_qwen2mlp_nd_s_kernel(tc, hidden_state, w_gate, w_up, w_down, out, impac
                     stop=(g == PASSES_2 - 1),
                 )
 
-        def store_out(half, copy):
+        def store_out(half):
             cols = slice(half * HALF_OUT, (half + 1) * HALF_OUT)
             out_sb = work.tile([P, HALF_OUT], F32, tag="out_sb")
-            copy(out=out_sb[:], in_=acc[("out", half)][:])
+            nc.vector.tensor_copy(out=out_sb[:], in_=acc[("out", half)][:])
             nc.sync.dma_start(out=out.rearrange("b s n -> (b s) n")[:, cols], in_=out_sb[:])
 
-        turn(("gate", 0))
         turn(("up", 0))
+        turn(("gate", 0))
         turn(("x", 0))
         turn(("gate", 1))
         turn(("up", 1))
+        square_up_rows(0)
         for c in range(CHUNKS):
+            square_up_rows(c + 1)
             empty(("gate", c), nc.scalar.copy)
             empty(("up", c), nc.vector.tensor_copy)
-            square_up_rows(c)
+            if c == 0:
+                empty(("x", 0), nc.vector.tensor_copy)
             pack(("gate", c))
             pack(("up", c))
             if c == 0:
-                empty(("x", 0), nc.scalar.copy)
                 pack(("x", 0))
             if c + 2 < CHUNKS:
                 turn(("gate", c + 2))
@@ -251,8 +239,8 @@ def tile_qwen2mlp_nd_s_kernel(tc, hidden_state, w_gate, w_up, w_down, out, impac
 
         silu(0)
         multiply(0)
-        square_up_rows(4)
-        square_up_rows(5)
+        square_up_rows(CHUNKS + 1)
+        square_up_rows(CHUNKS + 2)
         empty(("down", 0), nc.vector.tensor_copy)
         round_h(0)
         empty(("down", 1), nc.vector.tensor_copy)
@@ -267,9 +255,8 @@ def tile_qwen2mlp_nd_s_kernel(tc, hidden_state, w_gate, w_up, w_down, out, impac
         third_product(0)
         empty(("down", 2), nc.scalar.copy)
         square_h(1)
-        empty(("down", 3), nc.vector.tensor_copy)
-        square_up_rows(6)
-        square_up_rows(7)
+        empty(("down", 3), nc.scalar.copy)
+        square_up_rows(CHUNKS + 3)
         nc.scalar.activation(out=table_warm[:], in_=ones[:], func=ACT.Sqrt)
         sum_h_squares(0)
         pack(("down", 2))
@@ -288,8 +275,8 @@ def tile_qwen2mlp_nd_s_kernel(tc, hidden_state, w_gate, w_up, w_down, out, impac
         products_t = banks.tile([P, PACK, P], F32, tag="bank")
         for e in range(CHUNK_OPERANDS):
             nc.tensor.transpose(products_t[:, e, :], products[:, e, :], identity[:])
-        store_out(0, nc.scalar.copy)
-        store_out(1, nc.vector.tensor_copy)
+        store_out(0)
+        store_out(1)
         impacts_sb = keep.tile([P, P, CHUNK_OPERANDS], F32, name="impacts_sb")
         nc.scalar.activation(
             out=impacts_sb[:],

@@ -243,9 +243,9 @@ def tile_qwen2mlp_nd_s_kernel(tc, hidden_state, w_gate, w_up, w_down, out, impac
         square_up_rows(CHUNKS + 2)
         empty(("down", 0), nc.vector.tensor_copy)
         round_h(0)
-        empty(("down", 1), nc.vector.tensor_copy)
         silu(1)
         multiply(1)
+        empty(("down", 1), nc.scalar.copy)
         square_h(0)
         pack(("down", 0))
         round_h(1)

@@ -77,6 +77,12 @@ def tile_qwen2mlp_nd_s_kernel(tc, hidden_state, w_gate, w_up, w_down, out, impac
         for n in range(CHUNKS):
             load(("down", n), CHUNK_COLS, w_down.rearrange("(n r) k -> n r k", r=P)[n])
 
+        zeros = keep.tile([P, P], F32, name="zeros")
+        nc.vector.memset(zeros[:], 0.0)
+
+        def keep_warm(where, cols):
+            nc.tensor.matmul(where[:, 0:cols], lhsT=zeros[:], rhs=zeros[:, 0:cols], start=True, stop=True)
+
         identity = keep.tile([P, P], F32, name="identity")
         make_identity(nc, identity[:])
         ones = keep.tile([P, 1], F32, name="ones")
@@ -127,6 +133,9 @@ def tile_qwen2mlp_nd_s_kernel(tc, hidden_state, w_gate, w_up, w_down, out, impac
                 turned[key] = acc_pool.tile([P, PACK, P], F32, tag="acc", name="x_bank")
             else:
                 turned[key] = banks.tile([P, PACK, P], F32, tag="bank", name="%s_bank%d" % key)
+            if key == ("up", 0):
+                for n in range(5):
+                    keep_warm(turned[key][:, 0, :], P)
             turn_words(nc, turned[key], rows_of[key][:], identity[:])
 
         def empty(key, copy):
@@ -150,6 +159,8 @@ def tile_qwen2mlp_nd_s_kernel(tc, hidden_state, w_gate, w_up, w_down, out, impac
             for label in ("gate", "up"):
                 if u == 0:
                     acc[(label, g)] = acc_pool.tile([P, PACK, P], F32, tag="acc", name="%s_acc%d" % (label, g))
+                if label == "gate":
+                    keep_warm(acc[(label, g)][:, 2 * u, :], 96)
                 for e in range(CHUNK_OPERANDS):
                     cols = slice(e * P, (e + 1) * P)
                     nc.tensor.matmul_mx(

from contextlib import ExitStack

import concourse.mybir as mybir
from concourse.masks import make_identity

F32 = mybir.dt.float32
BF16 = mybir.dt.bfloat16
U32 = mybir.dt.uint32
U8 = mybir.dt.uint8
FP8X4 = mybir.dt.float8_e4m3fn_x4
ACT = mybir.ActivationFunctionType
ALU = mybir.AluOpType

P = 128
PACK = 4
K_PASS = P * PACK
BATCH = 4
HIDDEN = 512
INTER = 1024
PASSES_2 = INTER // K_PASS
CHUNK_OPERANDS = 2
CHUNK_COLS = CHUNK_OPERANDS * K_PASS
CHUNKS = 4
HALF_OUT = HIDDEN // 2
FLOPS = 2 * P * HIDDEN * INTER * 3


def turn_words(nc, bank, rows, identity):
    words = rows.bitcast(F32)
    for j in range(words.shape[1] // P):
        nc.tensor.transpose(bank[:, j, :], words[:, j * P : (j + 1) * P], identity)


def regroup(copy, stage, bank, operands):
    grouped = stage.tile([P, operands * K_PASS], BF16, tag="grouped", align_bytes=64)
    copy(
        out=grouped[:].bitcast(F32).rearrange("p (a r h) -> p a r h", a=operands, h=2),
        in_=bank[:, 0 : 2 * operands, :].rearrange("p (a h) r -> p a r h", h=2),
    )
    return grouped


def quantise(nc, grouped, pieces):
    cols = grouped.shape[1] // len(pieces)
    for j, (codes, scales) in enumerate(pieces):
        nc.vector.quantize_mx(
            out=codes.bitcast(FP8X4), scales=scales, in_=grouped[:, j * cols : (j + 1) * cols]
        )


def tile_qwen2mlp_nd_s_kernel(tc, hidden_state, w_gate, w_up, w_down, out, impacts):
    nc = tc.nc
    with ExitStack() as ctx:
        keep = ctx.enter_context(tc.tile_pool(name="keep", bufs=1))
        stage = ctx.enter_context(tc.tile_pool(name="stage", bufs=4))
        work = ctx.enter_context(tc.tile_pool(name="work", bufs=2))
        banks = ctx.enter_context(tc.psum_pool(name="banks", bufs=4))
        acc_pool = ctx.enter_context(tc.psum_pool(name="acc_pool", bufs=4))
        ctx.enter_context(tc.manual_schedule())

        rows_of = {}

        def load(key, cols, source):
            rows_of[key] = keep.tile([P, cols], BF16, name="%s_rows%d" % key)
            nc.sync.dma_start(out=rows_of[key][:], in_=source)

        def load_first(label, weight, c):
            chunks = weight.rearrange("(c m e) k -> c m (e k)", c=CHUNKS, e=CHUNK_OPERANDS)
            load((label, c), CHUNK_COLS, chunks[c])

        load_first("up", w_up, 0)
        load_first("gate", w_gate, 0)
        load(("x", 0), HIDDEN, hidden_state.rearrange("b s k -> (b s) k"))
        for c in range(1, CHUNKS):
            load_first("gate", w_gate, c)
            load_first("up", w_up, c)
        for n in range(CHUNKS):
            load(("down", n), CHUNK_COLS, w_down.rearrange("(n r) k -> n r k", r=P)[n])

        zeros = keep.tile([P, P], F32, name="zeros")
        nc.vector.memset(zeros[:], 0.0)

        def keep_warm(where, cols):
            nc.tensor.matmul(where[:, 0:cols], lhsT=zeros[:], rhs=zeros[:, 0:cols], start=True, stop=True)

        identity = keep.tile([P, P], F32, name="identity")
        make_identity(nc, identity[:])
        ones = keep.tile([P, 1], F32, name="ones")
        nc.vector.memset(ones[:], 1.0)
        products = keep.tile([P, CHUNK_OPERANDS, P], F32, name="products")
        nc.vector.memset(products[:], 0.0)
        table_warm = keep.tile([P, 1], F32, name="table_warm")
        nc.scalar.activation(out=table_warm[:], in_=ones[:], func=ACT.Silu)

        x_codes = keep.tile([P, P], U32, name="x_codes", align_bytes=64)
        x_scales = keep.tile([P, P], U8, name="x_scales", align_bytes=64)
        first_codes = {}
        first_scales = {}
        for label in ("gate", "up"):
            first_codes[label] = keep.tile(
                [P, CHUNKS, CHUNK_OPERANDS * P], U32, name="%s_codes" % label, align_bytes=64
            )
            first_scales[label] = keep.tile(
                [P, CHUNKS, CHUNK_OPERANDS * P], U8, name="%s_scales" % label, align_bytes=64
            )
        down_codes = keep.tile([P, PASSES_2, HIDDEN], U32, name="down_codes", align_bytes=64)
        down_scales = keep.tile([P, PASSES_2, HIDDEN], U8, name="down_scales", align_bytes=64)
        h_codes = keep.tile([P, PASSES_2, P], U32, name="h_codes", align_bytes=64)
        h_scales = keep.tile([P, PASSES_2, P], U8, name="h_scales", align_bytes=64)

        pieces_of = {("x", 0): [(x_codes[:], x_scales[:])]}
        for c in range(CHUNKS):
            for label in ("gate", "up"):
                pieces_of[(label, c)] = [(first_codes[label][:, c, :], first_scales[label][:, c, :])]
            cols = slice(c * P, (c + 1) * P)
            pieces_of[("down", c)] = [
                (down_codes[:, g, cols], down_scales[:, g, cols]) for g in range(PASSES_2)
            ]

        row_sq = keep.tile([P, CHUNKS * CHUNK_OPERANDS], F32, name="row_sq")
        h_sq_sum = keep.tile([P, PASSES_2, PACK * BATCH], F32, name="h_sq_sum")

        turned = {}
        grouped = {}
        acc = {}
        silu_gate = {}
        h_f32 = {}
        h_grouped = {}
        h_sq = {}

        def turn(key):
            if key == ("x", 0):
                turned[key] = acc_pool.tile([P, PACK, P], F32, tag="acc", name="x_bank")
            else:
                turned[key] = banks.tile([P, PACK, P], F32, tag="bank", name="%s_bank%d" % key)
            if key == ("up", 0):
                for n in range(5):
                    keep_warm(turned[key][:, 0, :], P)
            turn_words(nc, turned[key], rows_of[key][:], identity[:])

        def empty(key, copy):
            grouped[key] = regroup(copy, stage, turned[key], rows_of[key].shape[1] // K_PASS)

        def pack(key):
            quantise(nc, grouped[key], pieces_of[key])

        def square_up_rows(block):
            c, e = divmod(block, CHUNK_OPERANDS)
            squares = work.tile([P, K_PASS], F32, tag="squares")
            nc.scalar.activation(
                out=squares[:],
                in_=rows_of[("up", c)][:, e * K_PASS : (e + 1) * K_PASS],
                func=ACT.Square,
                accum_out=row_sq[:, block : block + 1],
            )

        def first_products(c):
            g, u = divmod(c, 2)
            for label in ("gate", "up"):
                if u == 0:
                    acc[(label, g)] = acc_pool.tile([P, PACK, P], F32, tag="acc", name="%s_acc%d" % (label, g))
                if label == "gate":
                    keep_warm(acc[(label, g)][:, 2 * u, :], 96)
                for e in range(CHUNK_OPERANDS):
                    cols = slice(e * P, (e + 1) * P)
                    nc.tensor.matmul_mx(
                        out=acc[(label, g)][:, 2 * u + e, :],
                        lhsT=first_codes[label][:, c, cols].bitcast(FP8X4),
                        lhsT_scale=first_scales[label][:, c, cols],
                        rhs=x_codes[:].bitcast(FP8X4),
                        rhs_scale=x_scales[:],
                        start=True,
                        stop=True,
                    )

        def silu(g):
            silu_gate[g] = work.tile([P, PACK, P], F32, tag="silu_gate", name="silu_gate%d" % g)
            nc.scalar.activation(out=silu_gate[g][:], in_=acc[("gate", g)][:], func=ACT.Silu)

        def multiply(g):
            h_f32[g] = work.tile([P, PACK, P], F32, tag="h_f32", name="h_f32_%d" % g)
            nc.vector.tensor_tensor(out=h_f32[g][:], in0=silu_gate[g][:], in1=acc[("up", g)][:], op=ALU.mult)

        def round_h(g):
            h_grouped[g] = work.tile([P, P, PACK], BF16, tag="h_grouped", name="h_grouped%d" % g, align_bytes=64)
            nc.vector.tensor_copy(out=h_grouped[g][:], in_=h_f32[g][:].rearrange("p t k -> p k t"))

        def pack_h(g):
            nc.vector.quantize_mx(
                out=h_codes[:, g, :].bitcast(FP8X4),
                scales=h_scales[:, g, :],
                in_=h_grouped[g][:].rearrange("p k t -> p (k t)"),
            )

        def square_h(g):
            h_sq[g] = work.tile([P, PACK, P], F32, tag="h_sq", name="h_sq%d" % g)
            nc.scalar.activation(out=h_sq[g][:], in_=h_f32[g][:], func=ACT.Square)

        def sum_h_squares(g):
            nc.vector.tensor_reduce(
                out=h_sq_sum[:, g, :],
                in_=h_sq[g][:].rearrange("p t (b s) -> p (t b) s", b=BATCH),
                axis=mybir.AxisListType.X,
                op=ALU.add,
            )

        def third_product(half):
            cols = slice(half * HALF_OUT, (half + 1) * HALF_OUT)
            acc[("out", half)] = acc_pool.tile([P, HALF_OUT], F32, tag="acc", name="out_acc%d" % half)
            for g in range(PASSES_2):
                nc.tensor.matmul_mx(
                    out=acc[("out", half)][:],
                    lhsT=h_codes[:, g, :].bitcast(FP8X4),
                    lhsT_scale=h_scales[:, g, :],
                    rhs=down_codes[:, g, cols].bitcast(FP8X4),
                    rhs_scale=down_scales[:, g, cols],
                    start=(g == 0),
                    stop=(g == PASSES_2 - 1),
                )

        def store_out(half):
            cols = slice(half * HALF_OUT, (half + 1) * HALF_OUT)
            out_sb = work.tile([P, HALF_OUT], F32, tag="out_sb")
            nc.vector.tensor_copy(out=out_sb[:], in_=acc[("out", half)][:])
            nc.sync.dma_start(out=out.rearrange("b s n -> (b s) n")[:, cols], in_=out_sb[:])

        turn(("up", 0))
        turn(("gate", 0))
        turn(("x", 0))
        turn(("gate", 1))
        turn(("up", 1))
        square_up_rows(0)
        for c in range(CHUNKS):
            square_up_rows(c + 1)
            empty(("gate", c), nc.scalar.copy)
            empty(("up", c), nc.vector.tensor_copy)
            if c == 0:
                empty(("x", 0), nc.vector.tensor_copy)
            pack(("gate", c))
            pack(("up", c))
            if c == 0:
                pack(("x", 0))
            if c + 2 < CHUNKS:
                turn(("gate", c + 2))
                turn(("up", c + 2))
            first_products(c)
            if c + 2 >= CHUNKS:
                turn(("down", 2 * (c + 2 - CHUNKS)))
                turn(("down", 2 * (c + 2 - CHUNKS) + 1))

        silu(0)
        multiply(0)
        square_up_rows(CHUNKS + 1)
        square_up_rows(CHUNKS + 2)
        empty(("down", 0), nc.vector.tensor_copy)
        round_h(0)
        silu(1)
        multiply(1)
        empty(("down", 1), nc.scalar.copy)
        square_h(0)
        pack(("down", 0))
        round_h(1)
        pack(("down", 1))
        pack_h(0)
        pack_h(1)
        third_product(0)
        empty(("down", 2), nc.scalar.copy)
        square_h(1)
        empty(("down", 3), nc.scalar.copy)
        square_up_rows(CHUNKS + 3)
        nc.scalar.activation(out=table_warm[:], in_=ones[:], func=ACT.Sqrt)
        sum_h_squares(0)
        pack(("down", 2))
        pack(("down", 3))
        third_product(1)
        sum_h_squares(1)
        nc.vector.tensor_tensor(
            out=products[:, :, 0 : BATCH * CHUNKS].rearrange("p e (b c) -> p e b c", b=BATCH),
            in0=h_sq_sum[:].rearrange("p g (u e b) -> p e b (g u)", u=2, e=CHUNK_OPERANDS),
            in1=row_sq[:]
            .rearrange("p (c e) -> p e c", e=CHUNK_OPERANDS)
            .unsqueeze(2)
            .to_broadcast([P, CHUNK_OPERANDS, BATCH, CHUNKS]),
            op=ALU.mult,
        )
        products_t = banks.tile([P, PACK, P], F32, tag="bank")
        for e in range(CHUNK_OPERANDS):
            nc.tensor.transpose(products_t[:, e, :], products[:, e, :], identity[:])
        store_out(0)
        store_out(1)
        impacts_sb = keep.tile([P, P, CHUNK_OPERANDS], F32, name="impacts_sb")
        nc.scalar.activation(
            out=impacts_sb[:],
            in_=products_t[:, 0:CHUNK_OPERANDS, :].rearrange("r e m -> r m e"),
            func=ACT.Sqrt,
        )
        nc.sync.dma_start(
            out=impacts.rearrange("b (c i) -> (b c) i", c=CHUNKS),
            in_=impacts_sb[0 : BATCH * CHUNKS].rearrange("r m e -> r (m e)"),
        )
